import numpy as np
import ml_dtypes


def mxq(x, axis, fmt="e4m3"):
    dtype, down = {"e4m3": (ml_dtypes.float8_e4m3fn, 7), "e5m2": (ml_dtypes.float8_e5m2, 14)}[fmt]
    v = np.moveaxis(np.asarray(x, np.float32).astype(ml_dtypes.bfloat16).astype(np.float64), axis, -1)
    blocks = v.reshape(v.shape[:-1] + (-1, 32))
    amax = np.abs(blocks).max(-1, keepdims=True)
    byte = np.maximum(np.where(amax > 0, np.frexp(amax)[1] - 1 + 127, 0) - down, 1)
    scale = np.exp2(byte - 127.0)
    codes = (blocks / scale).astype(np.float32).astype(dtype).astype(np.float64)
    return np.moveaxis((codes * scale).reshape(v.shape), -1, axis)


WIDE = False


def mx_kscale(k):
    if not WIDE:
        return np.ones(k)
    levels = np.array([30, -30])
    if k % 512:
        return np.exp2(np.random.permutation(np.resize(levels, k // 32))).repeat(32)
    a = np.empty((k // 512, 16))
    for p in range(k // 512):
        a[p, :8] = np.random.permutation(np.resize(levels, 8))
        for g in range(8):
            far = levels[np.abs(levels - a[p, g]) >= 10]
            a[p, g + 8] = far[np.random.randint(len(far))]
    return np.exp2(a.ravel()).repeat(32)


BF16 = ml_dtypes.bfloat16


def bf(x):
    return np.asarray(x, np.float32).astype(BF16)


def f64(x):
    return np.asarray(x).astype(np.float64)


E2M1 = np.array([0.0, 0.5, 1.0, 1.5, 2.0, 3.0, 4.0, 6.0, -0.0, -0.5, -1.0, -1.5, -2.0, -3.0, -4.0, -6.0])


def pack_weight(w, fmt):
    k, n = w.shape
    w = f64(bf(w)).reshape(k // 32, 32, n)
    amax = np.abs(w).max(1)
    if fmt == "e4m3":
        byte = np.frexp(amax)[1] - 1 + 127 - 7
    else:
        mant, ex = np.frexp(amax / 6.0)
        byte = np.where(mant > 0.5, ex, ex - 1) + 127
    byte = np.clip(np.where(amax > 0, byte, 1), 1, 254)
    scaled = (w * np.exp2(127.0 - byte)[:, None, :]).reshape(k, n).astype(np.float32)
    by_word = np.ascontiguousarray(scaled.reshape(k // 512, 128, 4, n).transpose(0, 1, 3, 2))
    if fmt == "e4m3":
        words = by_word.astype(ml_dtypes.float8_e4m3fn).view(np.uint8)
    else:
        c = by_word.astype(ml_dtypes.float4_e2m1fn).view(np.uint8) & 0xF
        words = c[..., 0::2] | (c[..., 1::2] << 4)
    return np.ascontiguousarray(words), np.ascontiguousarray(byte.astype(np.uint8).reshape(k // 512, 16, n))


def unpack_weight(words, scales, fmt):
    g, p, n, _ = words.shape
    if fmt == "e4m3":
        vals = np.ascontiguousarray(words).view(ml_dtypes.float8_e4m3fn).astype(np.float64)
    else:
        nib = np.empty((g, p, n, 4), np.uint8)
        nib[..., 0::2] = words & 0xF
        nib[..., 1::2] = words >> 4
        vals = E2M1[nib]
    vals = vals * np.repeat(np.exp2(scales.astype(np.float64) - 127.0), 8, axis=1)[..., None]
    return vals.transpose(0, 1, 3, 2).reshape(g * 512, n)

def pack4(w):
    words, scales = pack_weight(w, "e2m1")
    return words.reshape(words.shape[0], 128, -1), scales


def unpack4(words, scales):
    return unpack_weight(words.reshape(words.shape[0], 128, -1, 2), scales, "e2m1")


N, S, D, H = 4, 512, 1024, 8
L = N * S
DH = D // H


def rope(t, cos, sin):
    tr = t[..., 0::2]
    ti = t[..., 1::2]
    c = cos[:, None, :]
    s = sin[:, None, :]
    out_r = tr * c - ti * s
    out_i = tr * s + ti * c
    return np.stack([out_r, out_i], axis=-1).reshape(t.shape)


def setup_inputs():
    s = mx_kscale(D)
    ang = np.random.uniform(0.0, 2.0 * np.pi, (L, DH // 2))
    x = bf(np.random.standard_normal((L, D)) * s)
    words, scales = pack4(np.random.standard_normal((D, 2 * D)) * 1.5 / np.sqrt(D) / s[:, None])
    b_qk = bf(np.random.standard_normal(2 * D) * 0.1)
    return {"x": x,
            "w_qk_words": words, "w_qk_scales": scales,
            "b_qk": b_qk,
            "freqs_cos": bf(np.cos(ang)), "freqs_sin": bf(np.sin(ang))}


def reference(x, w_qk_words, w_qk_scales, b_qk, freqs_cos, freqs_sin):
    qk = (mxq(f64(x), 1, "e5m2") @ unpack4(w_qk_words, w_qk_scales)) + f64(b_qk)
    q, k = [t.reshape(L, H, DH) for t in np.split(qk, 2, axis=-1)]
    c, s = f64(freqs_cos), f64(freqs_sin)
    return rope(q, c, s), rope(k, c, s)

@@ -1,0 +1,294 @@
+from contextlib import ExitStack
+
+import concourse.mybir as mybir
+from concourse.masks import make_identity
+
+F32 = mybir.dt.float32
+BF16 = mybir.dt.bfloat16
+I32 = mybir.dt.int32
+U32 = mybir.dt.uint32
+U8 = mybir.dt.uint8
+E5M2X4 = mybir.dt.float8_e5m2_x4
+E2M1X4 = mybir.dt.float4_e2m1fn_x4
+ALU = mybir.AluOpType
+ACT = mybir.ActivationFunctionType
+
+P = 128
+TOKENS = 2048
+D = 1024
+CHANNELS = 2048
+PASSES = 2
+ROWS = TOKENS // P
+GROUP_ROWS = 4
+GROUPS = ROWS // GROUP_ROWS
+GROUP_TOKENS = GROUP_ROWS * P
+HEADS = CHANNELS // P
+QUAD = 4
+QUADS = HEADS // QUAD
+STEPS = GROUPS * QUADS
+PAIRS = P // 2
+SUM_BANKS = 3
+TURN_BANKS = 5
+
+FLOPS = 2 * TOKENS * D * CHANNELS
+
+
+def tile_moonvitvisiontower_pa_kernel(
+    tc, x, w_qk_words, w_qk_scales, b_qk, freqs_cos, freqs_sin, out_0, out_1
+):
+    nc = tc.nc
+    x_rows = x.rearrange("(p i) d -> p i d", i=ROWS)
+    outs = [o.rearrange("(p i) h d -> p i (h d)", i=ROWS) for o in (out_0, out_1)]
+
+    with ExitStack() as ctx:
+        keep = ctx.enter_context(tc.tile_pool(name="keep", bufs=1))
+        work = ctx.enter_context(tc.tile_pool(name="work", bufs=2))
+        psum = ctx.enter_context(tc.psum_pool(name="psum", bufs=1))
+        ctx.enter_context(tc.manual_schedule())
+
+        counters = {"sum": 0, "turn": 0}
+
+        def next_bank(kind, banks, shape, dtype):
+            n = counters[kind]
+            counters[kind] = n + 1
+            tag = "%s%d" % (kind, n % banks)
+            return psum.tile(shape, dtype, name=tag, tag=tag)
+
+        bias_rows = keep.tile([P, P], BF16)
+        nc.gpsimd.memset(bias_rows[:], 0.0)
+        ident_bf = keep.tile([P, P], BF16)
+        make_identity(nc, ident_bf[:])
+        ident = keep.tile([P, P], F32)
+        make_identity(nc, ident[:])
+        w_scale = keep.tile([P, PASSES, CHANNELS], U8, align_bytes=64)
+        nc.vector.memset(w_scale[:].rearrange("p g n -> p (g n)").bitcast(I32), 0)
+        sign = keep.tile([P, 2], F32)
+        nc.vector.memset(sign[:, 0:1], -1.0)
+        nc.vector.memset(sign[:, 1:2], 1.0)
+
+        nc.scalar.dma_start(out=bias_rows[0:HEADS, :], in_=b_qk.rearrange("(h c) -> h c", c=P))
+        x_raw = []
+
+        def load_row(i):
+            t = keep.tile([P, 1, D], BF16, name="x_first%d" % i)
+            nc.sync.dma_start(out=t[:], in_=x_rows[:, i : i + 1, :])
+            x_raw.append(t[:, 0, :])
+
+        load_row(0)
+        load_row(1)
+        for q in range(4):
+            nc.sync.dma_start(
+                out=w_scale[32 * q : 32 * q + 4, :, :].bitcast(I32),
+                in_=w_qk_scales[:, 4 * q : 4 * q + 4, :].rearrange("g r n -> r g n").bitcast(I32),
+            )
+        quad_bytes = 2 * QUAD * P
+        w_first = keep.tile([P, PASSES, quad_bytes], U8, align_bytes=64)
+        nc.sync.dma_start(
+            out=w_first[:].bitcast(I32),
+            in_=w_qk_words[:, :, 0:quad_bytes].rearrange("g p n -> p g n").bitcast(I32),
+        )
+        sin = keep.tile([P, ROWS * PAIRS], BF16)
+        nc.sync.dma_start(out=sin[:], in_=freqs_sin.rearrange("(p i) j -> p (i j)", i=ROWS))
+        load_row(2)
+        cos = keep.tile([P, ROWS * PAIRS], BF16)
+        nc.sync.dma_start(out=cos[:], in_=freqs_cos.rearrange("(p i) j -> p (i j)", i=ROWS))
+        load_row(3)
+        w_rest = keep.tile([P, PASSES, 2 * CHANNELS - quad_bytes], U8, align_bytes=64)
+        nc.sync.dma_start(
+            out=w_rest[:].bitcast(I32),
+            in_=w_qk_words[:, :, quad_bytes:].rearrange("g p n -> p g n").bitcast(I32),
+        )
+        for g in range(1, GROUPS):
+            t = keep.tile([P, GROUP_ROWS, D], BF16, name="x_group%d" % g)
+            nc.sync.dma_start(out=t[:], in_=x_rows[:, GROUP_ROWS * g : GROUP_ROWS * (g + 1), :])
+            x_raw.extend(t[:, i, :] for i in range(GROUP_ROWS))
+
+        def w_words(g, head):
+            if head < QUAD:
+                return w_first[:, g, 2 * P * head : 2 * P * (head + 1)]
+            return w_rest[:, g, 2 * P * (head - QUAD) : 2 * P * (head - QUAD + 1)]
+
+        bias_psum = next_bank("sum", SUM_BANKS, [P, P], BF16)
+        nc.tensor.transpose(bias_psum[:], bias_rows[:], ident_bf[:])
+        bias = keep.tile([P, HEADS], F32)
+        nc.scalar.activation(out=bias[:], in_=bias_psum[:, 0:HEADS], func=ACT.Identity)
+
+        grouped = {}
+        codes = {}
+        scales = {}
+        signed_sin = keep.tile([P, ROWS * PAIRS, 2], BF16)
+
+        def turn_x(row):
+            g, i = divmod(row, GROUP_ROWS)
+            if i == 0:
+                grouped[g] = work.tile([P, PASSES, GROUP_TOKENS, 2], F32, name="grouped", align_bytes=64)
+            words = x_raw[row].bitcast(F32)
+            bank = next_bank("sum", SUM_BANKS, [P, PASSES, 2, P], F32)
+            for c in range(PASSES):
+                for u in range(2):
+                    nc.tensor.transpose(bank[:, c, u, :], words[:, 256 * c + u : 256 * (c + 1) : 2], ident[:])
+            nc.scalar.copy(
+                out=grouped[g][:, :, P * i : P * (i + 1), :],
+                in_=bank[:].rearrange("p c u r -> p c r u"),
+            )
+
+        def new_codes(g):
+            codes[g] = work.tile([P, PASSES, GROUP_TOKENS], U32, name="codes", align_bytes=64)
+            scales[g] = work.tile([P, PASSES, GROUP_TOKENS], U8, name="scales", align_bytes=64)
+
+        def quantize(g):
+            new_codes(g)
+            nc.vector.quantize_mx(
+                out=codes[g][:].rearrange("p c r -> p (c r)").bitcast(E5M2X4),
+                scales=scales[g][:].rearrange("p c r -> p (c r)"),
+                in_=grouped[g][:].rearrange("p c r u -> p (c r u)").bitcast(BF16),
+            )
+
+        def quantize_row(i):
+            if i == 0:
+                new_codes(0)
+            cols = slice(P * i, P * (i + 1))
+            for c in range(PASSES):
+                nc.vector.quantize_mx(
+                    out=codes[0][:, c, cols].bitcast(E5M2X4),
+                    scales=scales[0][:, c, cols],
+                    in_=grouped[0][:, c, cols, :].rearrange("p r u -> p (r u)").bitcast(BF16),
+                )
+
+        def sign_sin(g):
+            cols = slice(GROUP_ROWS * PAIRS * g, GROUP_ROWS * PAIRS * (g + 1))
+            shape = [P, GROUP_ROWS * PAIRS, 2]
+            nc.vector.tensor_tensor(
+                out=signed_sin[:, cols, :],
+                in0=sin[:, cols].unsqueeze(2).to_broadcast(shape),
+                in1=sign[:].unsqueeze(1).to_broadcast(shape),
+                op=ALU.mult,
+            )
+
+        def mx_group(out, g, head, cols):
+            for c in range(PASSES):
+                nc.tensor.matmul_mx(
+                    out=out,
+                    lhsT=w_words(c, head).bitcast(E2M1X4),
+                    lhsT_scale=w_scale[:, c, P * head : P * (head + 1)],
+                    rhs=codes[g][:, c, cols].bitcast(E5M2X4),
+                    rhs_scale=scales[g][:, c, cols],
+                    start=(c == 0),
+                    stop=(c == PASSES - 1),
+                )
+
+        def add_bias(out, in_, head):
+            nc.scalar.activation(out=out, in_=in_, func=ACT.Identity, bias=bias[:, head : head + 1])
+
+        def project(g, head):
+            bank = next_bank("sum", SUM_BANKS, [P, GROUP_TOKENS], F32)
+            mx_group(bank[:], g, head, slice(0, GROUP_TOKENS))
+            biased = work.tile([P, GROUP_TOKENS], F32, name="biased", bufs=6)
+            add_bias(biased[:], bank[:], head)
+            return biased
+
+        def project_row(i):
+            bank = next_bank("sum", SUM_BANKS, [P, QUAD * P], F32)
+            for head in range(QUAD):
+                mx_group(bank[:, P * head : P * (head + 1)], 0, head, slice(P * i, P * (i + 1)))
+            biased = work.tile([P, QUAD * P], F32, name="biased", bufs=6)
+            for head in range(QUAD):
+                add_bias(biased[:, P * head : P * (head + 1)], bank[:, P * head : P * (head + 1)], head)
+            return biased
+
+        def turn_back(biased):
+            bank = next_bank("turn", TURN_BANKS, [P, 4, P], F32)
+            for i in range(4):
+                nc.tensor.transpose(bank[:, i, :], biased[:, P * i : P * (i + 1)], ident[:])
+            return bank
+
+        pair_shape = [P, 4, PAIRS, 2]
+
+        def multiply(bank, cos_view, sin_view, direct, crossed):
+            pairs = bank[:].rearrange("p i (j e) -> p i j e", e=2)
+            nc.vector.tensor_tensor(
+                out=direct.rearrange("p i (j e) -> p i j e", e=2), in0=pairs, in1=cos_view, op=ALU.mult
+            )
+            nc.vector.tensor_tensor(
+                out=crossed.rearrange("p i (j e) -> p i j e", e=2),
+                in0=pairs[:, :, :, ::-1],
+                in1=sin_view,
+                op=ALU.mult,
+            )
+
+        def product_tiles():
+            direct = work.tile([P, GROUP_ROWS * 2 * P], F32, name="direct", bufs=3)
+            crossed = work.tile([P, GROUP_ROWS * 2 * P], F32, name="crossed", bufs=3)
+            return direct, crossed
+
+        def store(step, result, cols):
+            g, quad = divmod(step, QUADS)
+            which, part = divmod(quad, 2)
+            first = QUAD * P * part
+            nc.sync.dma_start(
+                out=outs[which][:, GROUP_ROWS * g : GROUP_ROWS * (g + 1), first + cols.start : first + cols.stop],
+                in_=result[:, :, cols],
+            )
+
+        result = work.tile([P, GROUP_ROWS, QUAD * P], F32, name="result", bufs=4)
+        turn_x(0)
+        turn_x(1)
+        quantize_row(0)
+        quantize_row(1)
+        sign_sin(0)
+        for i in range(GROUP_ROWS):
+            biased = project_row(i)
+            turn_x(i + 2)
+            if i + 2 < GROUP_ROWS:
+                quantize_row(i + 2)
+            if i == 0:
+                for g in range(1, GROUPS):
+                    sign_sin(g)
+            bank = turn_back(biased)
+            if i % 2 == 0:
+                direct, crossed = product_tiles()
+            cols = slice(QUAD * P * (i % 2), QUAD * P * (i % 2 + 1))
+            row_cols = slice(PAIRS * i, PAIRS * (i + 1))
+            multiply(
+                bank,
+                cos[:, row_cols].unsqueeze(1).unsqueeze(3).to_broadcast(pair_shape),
+                signed_sin[:, row_cols, :].unsqueeze(1).to_broadcast(pair_shape),
+                direct[:, cols].rearrange("p (h c) -> p h c", c=P),
+                crossed[:, cols].rearrange("p (h c) -> p h c", c=P),
+            )
+            if i % 2 == 1:
+                nc.gpsimd.tensor_tensor(
+                    out=result[:, i - 1 : i + 1, :].rearrange("p i c -> p (i c)"),
+                    in0=direct[:],
+                    in1=crossed[:],
+                    op=ALU.add,
+                )
+        store(0, result, slice(0, QUAD * P))
+
+        for step in range(1, STEPS):
+            g, quad = divmod(step, QUADS)
+            last = step == STEPS - 1
+            biased = [project(g, QUAD * quad + k) for k in range(QUAD)]
+            if step + GROUP_ROWS + 1 < ROWS:
+                turn_x(step + GROUP_ROWS + 1)
+            banks = [turn_back(t) for t in biased]
+            group_cols = slice(GROUP_ROWS * PAIRS * g, GROUP_ROWS * PAIRS * (g + 1))
+            cos_view = cos[:, group_cols].rearrange("p (i j) -> p i j", j=PAIRS).unsqueeze(3).to_broadcast(pair_shape)
+            sin_view = signed_sin[:, group_cols, :].rearrange("p (i j) e -> p i j e", j=PAIRS)
+            result = work.tile([P, GROUP_ROWS, QUAD * P], F32, name="result", bufs=4)
+            for half in range(2):
+                direct, crossed = product_tiles()
+                direct = direct[:].rearrange("p (i c) -> p i c", i=GROUP_ROWS)
+                crossed = crossed[:].rearrange("p (i c) -> p i c", i=GROUP_ROWS)
+                for k in range(2):
+                    cols = slice(P * k, P * (k + 1))
+                    multiply(banks[2 * half + k], cos_view, sin_view, direct[:, :, cols], crossed[:, :, cols])
+                    if quad == QUADS - 2 and half == 1 and k == 0 and g + 1 < GROUPS:
+                        quantize(g + 1)
+                half_cols = slice(2 * P * half, 2 * P * (half + 1))
+                adder = nc.vector if last and half == 1 else nc.gpsimd
+                adder.tensor_tensor(out=result[:, :, half_cols], in0=direct, in1=crossed, op=ALU.add)
+                if last:
+                    store(step, result, half_cols)
+            if not last:
+                store(step, result, slice(0, QUAD * P))

@@ -27,8 +27,10 @@ QUAD = 4
 QUADS = HEADS // QUAD
 STEPS = GROUPS * QUADS
 PAIRS = P // 2
-SUM_BANKS = 3
-TURN_BANKS = 5
+SUM_BANKS = 4
+TURN_BANKS = 4
+DUOS = GROUPS * HEADS // 2
+VECTOR_ADDS = 2
 
 FLOPS = 2 * TOKENS * D * CHANNELS
 
@@ -93,20 +95,32 @@ def tile_moonvitvisiontower_pa_kernel(
         cos = keep.tile([P, ROWS * PAIRS], BF16)
         nc.sync.dma_start(out=cos[:], in_=freqs_cos.rearrange("(p i) j -> p (i j)", i=ROWS))
         load_row(3)
-        w_rest = keep.tile([P, PASSES, 2 * CHANNELS - quad_bytes], U8, align_bytes=64)
-        nc.sync.dma_start(
-            out=w_rest[:].bitcast(I32),
-            in_=w_qk_words[:, :, quad_bytes:].rearrange("g p n -> p g n").bitcast(I32),
-        )
-        for g in range(1, GROUPS):
+        w_tiles = [(0, w_first)]
+
+        def load_w(first_head, heads):
+            t = keep.tile([P, PASSES, 2 * P * heads], U8, name="w_from%d" % first_head, align_bytes=64)
+            nc.sync.dma_start(
+                out=t[:].bitcast(I32),
+                in_=w_qk_words[:, :, 2 * P * first_head : 2 * P * (first_head + heads)]
+                .rearrange("g p n -> p g n")
+                .bitcast(I32),
+            )
+            w_tiles.append((first_head, t))
+
+        def load_group(g):
             t = keep.tile([P, GROUP_ROWS, D], BF16, name="x_group%d" % g)
             nc.sync.dma_start(out=t[:], in_=x_rows[:, GROUP_ROWS * g : GROUP_ROWS * (g + 1), :])
             x_raw.extend(t[:, i, :] for i in range(GROUP_ROWS))
 
+        load_w(QUAD, QUAD)
+        load_group(1)
+        load_w(2 * QUAD, 2 * QUAD)
+        load_group(2)
+        load_group(3)
+
         def w_words(g, head):
-            if head < QUAD:
-                return w_first[:, g, 2 * P * head : 2 * P * (head + 1)]
-            return w_rest[:, g, 2 * P * (head - QUAD) : 2 * P * (head - QUAD + 1)]
+            first_head, t = [entry for entry in w_tiles if entry[0] <= head][-1]
+            return t[:, g, 2 * P * (head - first_head) : 2 * P * (head - first_head + 1)]
 
         bias_psum = next_bank("sum", SUM_BANKS, [P, P], BF16)
         nc.tensor.transpose(bias_psum[:], bias_rows[:], ident_bf[:])
@@ -118,17 +132,18 @@ def tile_moonvitvisiontower_pa_kernel(
         scales = {}
         signed_sin = keep.tile([P, ROWS * PAIRS, 2], BF16)
 
-        def turn_x(row):
+        def turn_x(row, first_pass, passes):
             g, i = divmod(row, GROUP_ROWS)
-            if i == 0:
+            if i == 0 and first_pass == 0:
                 grouped[g] = work.tile([P, PASSES, GROUP_TOKENS, 2], F32, name="grouped", align_bytes=64)
             words = x_raw[row].bitcast(F32)
-            bank = next_bank("sum", SUM_BANKS, [P, PASSES, 2, P], F32)
-            for c in range(PASSES):
+            bank = next_bank("sum", SUM_BANKS, [P, passes, 2, P], F32)
+            for c in range(passes):
+                first = 256 * (first_pass + c)
                 for u in range(2):
-                    nc.tensor.transpose(bank[:, c, u, :], words[:, 256 * c + u : 256 * (c + 1) : 2], ident[:])
+                    nc.tensor.transpose(bank[:, c, u, :], words[:, first + u : first + 256 : 2], ident[:])
             nc.scalar.copy(
-                out=grouped[g][:, :, P * i : P * (i + 1), :],
+                out=grouped[g][:, first_pass : first_pass + passes, P * i : P * (i + 1), :],
                 in_=bank[:].rearrange("p c u r -> p c r u"),
             )
 
@@ -216,79 +231,91 @@ def tile_moonvitvisiontower_pa_kernel(
                 op=ALU.mult,
             )
 
-        def product_tiles():
-            direct = work.tile([P, GROUP_ROWS * 2 * P], F32, name="direct", bufs=3)
-            crossed = work.tile([P, GROUP_ROWS * 2 * P], F32, name="crossed", bufs=3)
+        def product_tiles(width):
+            direct = work.tile([P, width], F32, name="direct", bufs=5)
+            crossed = work.tile([P, width], F32, name="crossed", bufs=5)
             return direct, crossed
 
-        def store(step, result, cols):
-            g, quad = divmod(step, QUADS)
-            which, part = divmod(quad, 2)
-            first = QUAD * P * part
-            nc.sync.dma_start(
-                out=outs[which][:, GROUP_ROWS * g : GROUP_ROWS * (g + 1), first + cols.start : first + cols.stop],
-                in_=result[:, :, cols],
-            )
+        def add_and_store(engine, direct, crossed, rows, first_head, heads):
+            result = work.tile([P, rows.stop - rows.start, heads * P], F32, name="result", bufs=6)
+            engine.tensor_tensor(out=result[:], in0=direct, in1=crossed, op=ALU.add)
+            which, head = divmod(first_head, HEADS // 2)
+            nc.sync.dma_start(out=outs[which][:, rows, P * head : P * (head + heads)], in_=result[:])
 
-        result = work.tile([P, GROUP_ROWS, QUAD * P], F32, name="result", bufs=4)
-        turn_x(0)
-        turn_x(1)
-        quantize_row(0)
-        quantize_row(1)
-        sign_sin(0)
-        for i in range(GROUP_ROWS):
-            biased = project_row(i)
-            turn_x(i + 2)
-            if i + 2 < GROUP_ROWS:
-                quantize_row(i + 2)
-            if i == 0:
-                for g in range(1, GROUPS):
-                    sign_sin(g)
+        def finish_row(i, biased):
             bank = turn_back(biased)
-            if i % 2 == 0:
-                direct, crossed = product_tiles()
-            cols = slice(QUAD * P * (i % 2), QUAD * P * (i % 2 + 1))
+            direct, crossed = product_tiles(QUAD * P)
             row_cols = slice(PAIRS * i, PAIRS * (i + 1))
             multiply(
                 bank,
                 cos[:, row_cols].unsqueeze(1).unsqueeze(3).to_broadcast(pair_shape),
                 signed_sin[:, row_cols, :].unsqueeze(1).to_broadcast(pair_shape),
-                direct[:, cols].rearrange("p (h c) -> p h c", c=P),
-                crossed[:, cols].rearrange("p (h c) -> p h c", c=P),
+                direct[:].rearrange("p (h c) -> p h c", c=P),
+                crossed[:].rearrange("p (h c) -> p h c", c=P),
             )
-            if i % 2 == 1:
-                nc.gpsimd.tensor_tensor(
-                    out=result[:, i - 1 : i + 1, :].rearrange("p i c -> p (i c)"),
-                    in0=direct[:],
-                    in1=crossed[:],
-                    op=ALU.add,
-                )
-        store(0, result, slice(0, QUAD * P))
+            add_and_store(nc.gpsimd, direct[:].unsqueeze(1), crossed[:].unsqueeze(1), slice(i, i + 1), 0, QUAD)
 
-        for step in range(1, STEPS):
-            g, quad = divmod(step, QUADS)
-            last = step == STEPS - 1
-            biased = [project(g, QUAD * quad + k) for k in range(QUAD)]
-            if step + GROUP_ROWS + 1 < ROWS:
-                turn_x(step + GROUP_ROWS + 1)
+        left_over = []
+
+        def finish_duo(duo, biased):
+            g, first_head = divmod(2 * duo, HEADS)
             banks = [turn_back(t) for t in biased]
-            group_cols = slice(GROUP_ROWS * PAIRS * g, GROUP_ROWS * PAIRS * (g + 1))
+            rows = slice(GROUP_ROWS * g, GROUP_ROWS * (g + 1))
+            group_cols = slice(PAIRS * rows.start, PAIRS * rows.stop)
             cos_view = cos[:, group_cols].rearrange("p (i j) -> p i j", j=PAIRS).unsqueeze(3).to_broadcast(pair_shape)
             sin_view = signed_sin[:, group_cols, :].rearrange("p (i j) e -> p i j e", j=PAIRS)
-            result = work.tile([P, GROUP_ROWS, QUAD * P], F32, name="result", bufs=4)
-            for half in range(2):
-                direct, crossed = product_tiles()
-                direct = direct[:].rearrange("p (i c) -> p i c", i=GROUP_ROWS)
-                crossed = crossed[:].rearrange("p (i c) -> p i c", i=GROUP_ROWS)
-                for k in range(2):
-                    cols = slice(P * k, P * (k + 1))
-                    multiply(banks[2 * half + k], cos_view, sin_view, direct[:, :, cols], crossed[:, :, cols])
-                    if quad == QUADS - 2 and half == 1 and k == 0 and g + 1 < GROUPS:
-                        quantize(g + 1)
-                half_cols = slice(2 * P * half, 2 * P * (half + 1))
-                adder = nc.vector if last and half == 1 else nc.gpsimd
-                adder.tensor_tensor(out=result[:, :, half_cols], in0=direct, in1=crossed, op=ALU.add)
-                if last:
-                    store(step, result, half_cols)
-            if not last:
-                store(step, result, slice(0, QUAD * P))
+            direct, crossed = product_tiles(GROUP_ROWS * 2 * P)
+            direct = direct[:].rearrange("p (i c) -> p i c", i=GROUP_ROWS)
+            crossed = crossed[:].rearrange("p (i c) -> p i c", i=GROUP_ROWS)
+            for k in range(2):
+                cols = slice(P * k, P * (k + 1))
+                multiply(banks[k], cos_view, sin_view, direct[:, :, cols], crossed[:, :, cols])
+            if first_head == HEADS - 8 and g + 1 < GROUPS:
+                quantize(g + 1)
+            if duo < DUOS - VECTOR_ADDS:
+                add_and_store(nc.gpsimd, direct, crossed, rows, first_head, 2)
+            else:
+                left_over.append((direct, crossed, rows, first_head))
+
+        turn_x(0, 0, PASSES)
+        turn_x(1, 0, PASSES)
+        quantize_row(0)
+        quantize_row(1)
+        sign_sin(0)
+        biased = project_row(0)
+        turn_x(2, 0, PASSES)
+        quantize_row(2)
+        for g in range(1, GROUPS):
+            sign_sin(g)
+        finish_row(0, biased)
+        biased = project_row(1)
+        turn_x(3, 0, PASSES)
+        quantize_row(3)
+        for i in range(2, GROUP_ROWS):
+            ahead = project_row(i)
+            finish_row(i - 1, biased)
+            biased = ahead
+        turn_x(GROUP_ROWS, 0, PASSES)
+
+        half_rows = [(row, c) for row in range(GROUP_ROWS + 1, ROWS) for c in range(PASSES)]
+        for duo in range(QUAD // 2, DUOS):
+            g, first_head = divmod(2 * duo, HEADS)
+            ahead = [project(g, first_head + k) for k in range(2)]
+            if duo < QUAD:
+                row = half_rows[0][0]
+                half_rows = half_rows[PASSES:]
+                turn_x(row, 0, PASSES)
+            elif half_rows:
+                row, c = half_rows[0]
+                half_rows = half_rows[1:]
+                turn_x(row, c, 1)
+            if duo == QUAD // 2:
+                finish_row(GROUP_ROWS - 1, biased)
+            else:
+                finish_duo(duo - 1, biased)
+            biased = ahead
+        finish_duo(DUOS - 1, biased)
+        for direct, crossed, rows, first_head in left_over:
+            for k in range(2):
+                cols = slice(P * k, P * (k + 1))
+                add_and_store(nc.vector, direct[:, :, cols], crossed[:, :, cols], rows, first_head + k, 1)

@@ -62,6 +62,10 @@ def tile_moonvitvisiontower_pa_kernel(
         make_identity(nc, ident_bf[:])
         ident = keep.tile([P, P], F32)
         make_identity(nc, ident[:])
+        split = keep.tile([P, P], F32)
+        nc.gpsimd.tensor_copy(
+            out=split[:].rearrange("p (e j) -> p e j", e=2), in_=ident[:].rearrange("p (j e) -> p e j", e=2)
+        )
         w_scale = keep.tile([P, PASSES, CHANNELS], U8, align_bytes=64)
         nc.vector.memset(w_scale[:].rearrange("p g n -> p (g n)").bitcast(I32), 0)
         sign = keep.tile([P, 2], F32)
@@ -131,6 +135,7 @@ def tile_moonvitvisiontower_pa_kernel(
         codes = {}
         scales = {}
         signed_sin = keep.tile([P, ROWS * PAIRS, 2], BF16)
+        double_cos = keep.tile([P, ROWS * PAIRS, 2], BF16)
 
         def turn_x(row, first_pass, passes):
             g, i = divmod(row, GROUP_ROWS)
@@ -180,6 +185,10 @@ def tile_moonvitvisiontower_pa_kernel(
                 op=ALU.mult,
             )
 
+        def repeat_cos(g, copy):
+            cols = slice(GROUP_ROWS * PAIRS * g, GROUP_ROWS * PAIRS * (g + 1))
+            copy(out=double_cos[:, cols, :], in_=cos[:, cols].unsqueeze(2).to_broadcast([P, GROUP_ROWS * PAIRS, 2]))
+
         def mx_group(out, g, head, cols):
             for c in range(PASSES):
                 nc.tensor.matmul_mx(
@@ -214,13 +223,13 @@ def tile_moonvitvisiontower_pa_kernel(
         def turn_back(biased):
             bank = next_bank("turn", TURN_BANKS, [P, 4, P], F32)
             for i in range(4):
-                nc.tensor.transpose(bank[:, i, :], biased[:, P * i : P * (i + 1)], ident[:])
+                nc.tensor.transpose(bank[:, i, :], biased[:, P * i : P * (i + 1)], split[:])
             return bank
 
         pair_shape = [P, 4, PAIRS, 2]
 
         def multiply(bank, cos_view, sin_view, direct, crossed):
-            pairs = bank[:].rearrange("p i (j e) -> p i j e", e=2)
+            pairs = bank[:].rearrange("p i (e j) -> p i j e", e=2)
             nc.vector.tensor_tensor(
                 out=direct.rearrange("p i (j e) -> p i j e", e=2), in0=pairs, in1=cos_view, op=ALU.mult
             )
@@ -248,7 +257,7 @@ def tile_moonvitvisiontower_pa_kernel(
             row_cols = slice(PAIRS * i, PAIRS * (i + 1))
             multiply(
                 bank,
-                cos[:, row_cols].unsqueeze(1).unsqueeze(3).to_broadcast(pair_shape),
+                double_cos[:, row_cols, :].unsqueeze(1).to_broadcast(pair_shape),
                 signed_sin[:, row_cols, :].unsqueeze(1).to_broadcast(pair_shape),
                 direct[:].rearrange("p (h c) -> p h c", c=P),
                 crossed[:].rearrange("p (h c) -> p h c", c=P),
@@ -262,7 +271,7 @@ def tile_moonvitvisiontower_pa_kernel(
             banks = [turn_back(t) for t in biased]
             rows = slice(GROUP_ROWS * g, GROUP_ROWS * (g + 1))
             group_cols = slice(PAIRS * rows.start, PAIRS * rows.stop)
-            cos_view = cos[:, group_cols].rearrange("p (i j) -> p i j", j=PAIRS).unsqueeze(3).to_broadcast(pair_shape)
+            cos_view = double_cos[:, group_cols, :].rearrange("p (i j) e -> p i j e", j=PAIRS)
             sin_view = signed_sin[:, group_cols, :].rearrange("p (i j) e -> p i j e", j=PAIRS)
             direct, crossed = product_tiles(GROUP_ROWS * 2 * P)
             direct = direct[:].rearrange("p (i c) -> p i c", i=GROUP_ROWS)
@@ -285,6 +294,7 @@ def tile_moonvitvisiontower_pa_kernel(
         biased = project_row(0)
         turn_x(2, 0, PASSES)
         quantize_row(2)
+        repeat_cos(0, nc.vector.tensor_copy)
         for g in range(1, GROUPS):
             sign_sin(g)
         finish_row(0, biased)
@@ -309,6 +319,8 @@ def tile_moonvitvisiontower_pa_kernel(
                 row, c = half_rows[0]
                 half_rows = half_rows[1:]
                 turn_x(row, c, 1)
+            if first_head == HEADS - 4 and g + 1 < GROUPS:
+                repeat_cos(g + 1, nc.scalar.copy)
             if duo == QUAD // 2:
                 finish_row(GROUP_ROWS - 1, biased)
             else:

@@ -39,8 +39,8 @@ def tile_moonvitvisiontower_pa_kernel(
     tc, x, w_qk_words, w_qk_scales, b_qk, freqs_cos, freqs_sin, out_0, out_1
 ):
     nc = tc.nc
-    x_rows = x.rearrange("(p i) d -> p i d", i=ROWS)
-    outs = [o.rearrange("(p i) h d -> p i (h d)", i=ROWS) for o in (out_0, out_1)]
+    x_rows = x.rearrange("(g p i) d -> g p i d", p=P, i=GROUP_ROWS)
+    outs = [o.rearrange("(g p i) h d -> g p i (h d)", p=P, i=GROUP_ROWS) for o in (out_0, out_1)]
 
     with ExitStack() as ctx:
         keep = ctx.enter_context(tc.tile_pool(name="keep", bufs=1))
@@ -77,7 +77,7 @@ def tile_moonvitvisiontower_pa_kernel(
 
         def load_row(i):
             t = keep.tile([P, 1, D], BF16, name="x_first%d" % i)
-            nc.sync.dma_start(out=t[:], in_=x_rows[:, i : i + 1, :])
+            nc.sync.dma_start(out=t[:], in_=x_rows[0, :, i : i + 1, :])
             x_raw.append(t[:, 0, :])
 
         load_row(0)
@@ -94,10 +94,16 @@ def tile_moonvitvisiontower_pa_kernel(
             in_=w_qk_words[:, :, 0:quad_bytes].rearrange("g p n -> p g n").bitcast(I32),
         )
         sin = keep.tile([P, ROWS * PAIRS], BF16)
-        nc.sync.dma_start(out=sin[:], in_=freqs_sin.rearrange("(p i) j -> p (i j)", i=ROWS))
+        nc.sync.dma_start(
+            out=sin[:].rearrange("p (g c) -> p g c", g=GROUPS),
+            in_=freqs_sin.rearrange("(g p i) j -> p g (i j)", p=P, i=GROUP_ROWS),
+        )
         load_row(2)
         cos = keep.tile([P, ROWS * PAIRS], BF16)
-        nc.sync.dma_start(out=cos[:], in_=freqs_cos.rearrange("(p i) j -> p (i j)", i=ROWS))
+        nc.sync.dma_start(
+            out=cos[:].rearrange("p (g c) -> p g c", g=GROUPS),
+            in_=freqs_cos.rearrange("(g p i) j -> p g (i j)", p=P, i=GROUP_ROWS),
+        )
         load_row(3)
         w_tiles = [(0, w_first)]
 
@@ -113,7 +119,7 @@ def tile_moonvitvisiontower_pa_kernel(
 
         def load_group(g):
             t = keep.tile([P, GROUP_ROWS, D], BF16, name="x_group%d" % g)
-            nc.sync.dma_start(out=t[:], in_=x_rows[:, GROUP_ROWS * g : GROUP_ROWS * (g + 1), :])
+            nc.sync.dma_start(out=t[:], in_=x_rows[g])
             x_raw.extend(t[:, i, :] for i in range(GROUP_ROWS))
 
         load_w(QUAD, QUAD)
@@ -185,6 +191,11 @@ def tile_moonvitvisiontower_pa_kernel(
                 op=ALU.mult,
             )
 
+        def sign_sin_on_scalar(g):
+            cols = slice(GROUP_ROWS * PAIRS * g, GROUP_ROWS * PAIRS * (g + 1))
+            nc.scalar.activation(out=signed_sin[:, cols, 0], in_=sin[:, cols], func=ACT.Copy, scale=-1.0)
+            nc.scalar.copy(out=signed_sin[:, cols, 1], in_=sin[:, cols])
+
         def repeat_cos(g, copy):
             cols = slice(GROUP_ROWS * PAIRS * g, GROUP_ROWS * PAIRS * (g + 1))
             copy(out=double_cos[:, cols, :], in_=cos[:, cols].unsqueeze(2).to_broadcast([P, GROUP_ROWS * PAIRS, 2]))
@@ -245,11 +256,20 @@ def tile_moonvitvisiontower_pa_kernel(
             crossed = work.tile([P, width], F32, name="crossed", bufs=5)
             return direct, crossed
 
-        def add_and_store(engine, direct, crossed, rows, first_head, heads):
-            result = work.tile([P, rows.stop - rows.start, heads * P], F32, name="result", bufs=6)
-            engine.tensor_tensor(out=result[:], in0=direct, in1=crossed, op=ALU.add)
+        results = {}
+
+        def add(engine, direct, crossed, g, rows, first_head, heads):
             which, head = divmod(first_head, HEADS // 2)
-            nc.sync.dma_start(out=outs[which][:, rows, P * head : P * (head + heads)], in_=result[:])
+            if (g, which) not in results:
+                results[(g, which)] = work.tile([P, GROUP_ROWS, D], F32, name="result", bufs=3)
+            engine.tensor_tensor(
+                out=results[(g, which)][:, rows, P * head : P * (head + heads)], in0=direct, in1=crossed, op=ALU.add
+            )
+
+        def store(g, first_head, heads):
+            which, head = divmod(first_head, HEADS // 2)
+            cols = slice(P * head, P * (head + heads))
+            nc.sync.dma_start(out=outs[which][g, :, :, cols], in_=results[(g, which)][:, :, cols])
 
         def finish_row(i, biased):
             bank = turn_back(biased)
@@ -262,7 +282,7 @@ def tile_moonvitvisiontower_pa_kernel(
                 direct[:].rearrange("p (h c) -> p h c", c=P),
                 crossed[:].rearrange("p (h c) -> p h c", c=P),
             )
-            add_and_store(nc.gpsimd, direct[:].unsqueeze(1), crossed[:].unsqueeze(1), slice(i, i + 1), 0, QUAD)
+            add(nc.gpsimd, direct[:].unsqueeze(1), crossed[:].unsqueeze(1), 0, slice(i, i + 1), 0, QUAD)
 
         left_over = []
 
@@ -282,21 +302,23 @@ def tile_moonvitvisiontower_pa_kernel(
             if first_head == HEADS - 8 and g + 1 < GROUPS:
                 quantize(g + 1)
             if duo < DUOS - VECTOR_ADDS:
-                add_and_store(nc.gpsimd, direct, crossed, rows, first_head, 2)
+                add(nc.gpsimd, direct, crossed, g, slice(0, GROUP_ROWS), first_head, 2)
+                if duo >= DUOS - QUAD:
+                    store(g, first_head, 2)
+                elif duo % QUAD == QUAD - 1:
+                    store(g, first_head + 2 - HEADS // 2, HEADS // 2)
             else:
-                left_over.append((direct, crossed, rows, first_head))
+                left_over.append((direct, crossed, first_head))
 
         turn_x(0, 0, PASSES)
         turn_x(1, 0, PASSES)
         quantize_row(0)
         quantize_row(1)
         sign_sin(0)
+        repeat_cos(0, nc.vector.tensor_copy)
         biased = project_row(0)
         turn_x(2, 0, PASSES)
         quantize_row(2)
-        repeat_cos(0, nc.vector.tensor_copy)
-        for g in range(1, GROUPS):
-            sign_sin(g)
         finish_row(0, biased)
         biased = project_row(1)
         turn_x(3, 0, PASSES)
@@ -321,13 +343,16 @@ def tile_moonvitvisiontower_pa_kernel(
                 turn_x(row, c, 1)
             if first_head == HEADS - 4 and g + 1 < GROUPS:
                 repeat_cos(g + 1, nc.scalar.copy)
+            if first_head == HEADS - 2 and g + 1 < GROUPS:
+                sign_sin_on_scalar(g + 1)
             if duo == QUAD // 2:
                 finish_row(GROUP_ROWS - 1, biased)
             else:
                 finish_duo(duo - 1, biased)
             biased = ahead
         finish_duo(DUOS - 1, biased)
-        for direct, crossed, rows, first_head in left_over:
+        for direct, crossed, first_head in left_over:
             for k in range(2):
                 cols = slice(P * k, P * (k + 1))
-                add_and_store(nc.vector, direct[:, :, cols], crossed[:, :, cols], rows, first_head + k, 1)
+                add(nc.vector, direct[:, :, cols], crossed[:, :, cols], GROUPS - 1, slice(0, GROUP_ROWS), first_head + k, 1)
+                store(GROUPS - 1, first_head + k, 1)

@@ -30,7 +30,7 @@ PAIRS = P // 2
 SUM_BANKS = 4
 TURN_BANKS = 4
 DUOS = GROUPS * HEADS // 2
-VECTOR_ADDS = 2
+SUMMED_TAIL = 2
 
 FLOPS = 2 * TOKENS * D * CHANNELS
 
@@ -66,11 +66,14 @@ def tile_moonvitvisiontower_pa_kernel(
         nc.gpsimd.tensor_copy(
             out=split[:].rearrange("p (e j) -> p e j", e=2), in_=ident[:].rearrange("p (j e) -> p e j", e=2)
         )
+        swap = keep.tile([P, P], F32)
+        for e in range(2):
+            nc.gpsimd.tensor_copy(out=swap[:, e:P:2], in_=ident[:, 1 - e : P : 2])
         w_scale = keep.tile([P, PASSES, CHANNELS], U8, align_bytes=64)
         nc.vector.memset(w_scale[:].rearrange("p g n -> p (g n)").bitcast(I32), 0)
         sign = keep.tile([P, 2], F32)
-        nc.vector.memset(sign[:, 0:1], -1.0)
-        nc.vector.memset(sign[:, 1:2], 1.0)
+        nc.vector.memset(sign[:, 0:1], 1.0)
+        nc.vector.memset(sign[:, 1:2], -1.0)
 
         nc.scalar.dma_start(out=bias_rows[0:HEADS, :], in_=b_qk.rearrange("(h c) -> h c", c=P))
         x_raw = []
@@ -158,6 +161,21 @@ def tile_moonvitvisiontower_pa_kernel(
                 in_=bank[:].rearrange("p c u r -> p c r u"),
             )
 
+        def sort_words(row, c):
+            words = x_raw[row].bitcast(F32)[:, 256 * c : 256 * (c + 1)]
+            sorted_words = work.tile([P, 2, P], F32, name="sorted_words", bufs=3)
+            nc.scalar.copy(out=sorted_words[:], in_=words.rearrange("p (k u) -> p u k", u=2))
+            return sorted_words
+
+        def turn_sorted(row, c, sorted_words):
+            g, i = divmod(row, GROUP_ROWS)
+            if i == 0 and c == 0:
+                grouped[g] = work.tile([P, PASSES, GROUP_TOKENS, 2], F32, name="grouped", align_bytes=64)
+            bank = next_bank("sum", SUM_BANKS, [P, 2, P], F32)
+            for u in range(2):
+                nc.tensor.transpose(bank[:, u, :], sorted_words[:, u, :], ident[:])
+            nc.scalar.copy(out=grouped[g][:, c, P * i : P * (i + 1), :], in_=bank[:].rearrange("p u r -> p r u"))
+
         def new_codes(g):
             codes[g] = work.tile([P, PASSES, GROUP_TOKENS], U32, name="codes", align_bytes=64)
             scales[g] = work.tile([P, PASSES, GROUP_TOKENS], U8, name="scales", align_bytes=64)
@@ -193,8 +211,8 @@ def tile_moonvitvisiontower_pa_kernel(
 
         def sign_sin_on_scalar(g):
             cols = slice(GROUP_ROWS * PAIRS * g, GROUP_ROWS * PAIRS * (g + 1))
-            nc.scalar.activation(out=signed_sin[:, cols, 0], in_=sin[:, cols], func=ACT.Copy, scale=-1.0)
-            nc.scalar.copy(out=signed_sin[:, cols, 1], in_=sin[:, cols])
+            nc.scalar.copy(out=signed_sin[:, cols, 0], in_=sin[:, cols])
+            nc.scalar.activation(out=signed_sin[:, cols, 1], in_=sin[:, cols], func=ACT.Copy, scale=-1.0)
 
         def repeat_cos(g, copy):
             cols = slice(GROUP_ROWS * PAIRS * g, GROUP_ROWS * PAIRS * (g + 1))
@@ -214,6 +232,39 @@ def tile_moonvitvisiontower_pa_kernel(
 
         def add_bias(out, in_, head):
             nc.scalar.activation(out=out, in_=in_, func=ACT.Identity, bias=bias[:, head : head + 1])
+
+        turned_tables = {}
+
+        def turn_tables(g):
+            bank = next_bank("sum", SUM_BANKS, [P, 2, GROUP_ROWS, P], BF16)
+            for n, table in enumerate((double_cos, signed_sin)):
+                for i in range(GROUP_ROWS):
+                    row = GROUP_ROWS * g + i
+                    nc.tensor.transpose(
+                        bank[:, n, i, :],
+                        table[:, PAIRS * row : PAIRS * (row + 1), :].rearrange("p j e -> p (j e)"),
+                        ident_bf[:],
+                    )
+            turned_tables[g] = work.tile([P, 2, GROUP_TOKENS], BF16, name="turned_table")
+            nc.scalar.copy(out=turned_tables[g][:], in_=bank[:].rearrange("p n i r -> p n (i r)"))
+
+        def summed_on_tensor(duo, k):
+            return duo >= DUOS - SUMMED_TAIL or (duo >= HEADS // 2 and duo % 2 == 1 and k == 1)
+
+        def project_and_multiply(g, head):
+            bank = next_bank("sum", SUM_BANKS, [P, GROUP_TOKENS], F32)
+            mx_group(bank[:], g, head, slice(0, GROUP_TOKENS))
+            products = work.tile([P, 2, GROUP_TOKENS], F32, name="products", bufs=4)
+            for n in range(2):
+                nc.vector.scalar_tensor_tensor(
+                    out=products[:, n, :],
+                    in0=bank[:],
+                    scalar=bias[:, head : head + 1],
+                    in1=turned_tables[g][:, n, :],
+                    op0=ALU.add,
+                    op1=ALU.mult,
+                )
+            return products
 
         def project(g, head):
             bank = next_bank("sum", SUM_BANKS, [P, GROUP_TOKENS], F32)
@@ -258,13 +309,30 @@ def tile_moonvitvisiontower_pa_kernel(
 
         results = {}
 
-        def add(engine, direct, crossed, g, rows, first_head, heads):
+        def result_view(g, rows, first_head, heads):
             which, head = divmod(first_head, HEADS // 2)
             if (g, which) not in results:
                 results[(g, which)] = work.tile([P, GROUP_ROWS, D], F32, name="result", bufs=3)
-            engine.tensor_tensor(
-                out=results[(g, which)][:, rows, P * head : P * (head + heads)], in0=direct, in1=crossed, op=ALU.add
+            return results[(g, which)][:, rows, P * head : P * (head + heads)]
+
+        def combine(direct, crossed, g, rows, first_head, heads):
+            nc.gpsimd.tensor_tensor(
+                out=result_view(g, rows, first_head, heads), in0=direct, in1=crossed, op=ALU.subtract
             )
+
+        def turn_and_sum(products, g, head):
+            bank = next_bank("turn", TURN_BANKS, [P, GROUP_ROWS, P], F32)
+            for i in range(GROUP_ROWS):
+                for n, order in enumerate((ident, swap)):
+                    nc.tensor.matmul(
+                        out=bank[:, i, :],
+                        lhsT=products[:, n, P * i : P * (i + 1)],
+                        rhs=order[:],
+                        start=(n == 0),
+                        stop=(n == 1),
+                        is_transpose=True,
+                    )
+            nc.scalar.copy(out=result_view(g, slice(0, GROUP_ROWS), head, 1), in_=bank[:])
 
         def store(g, first_head, heads):
             which, head = divmod(first_head, HEADS // 2)
@@ -282,33 +350,33 @@ def tile_moonvitvisiontower_pa_kernel(
                 direct[:].rearrange("p (h c) -> p h c", c=P),
                 crossed[:].rearrange("p (h c) -> p h c", c=P),
             )
-            add(nc.gpsimd, direct[:].unsqueeze(1), crossed[:].unsqueeze(1), 0, slice(i, i + 1), 0, QUAD)
+            combine(direct[:].unsqueeze(1), crossed[:].unsqueeze(1), 0, slice(i, i + 1), 0, QUAD)
 
-        left_over = []
-
-        def finish_duo(duo, biased):
+        def finish_duo(duo, projected):
             g, first_head = divmod(2 * duo, HEADS)
-            banks = [turn_back(t) for t in biased]
-            rows = slice(GROUP_ROWS * g, GROUP_ROWS * (g + 1))
-            group_cols = slice(PAIRS * rows.start, PAIRS * rows.stop)
-            cos_view = double_cos[:, group_cols, :].rearrange("p (i j) e -> p i j e", j=PAIRS)
-            sin_view = signed_sin[:, group_cols, :].rearrange("p (i j) e -> p i j e", j=PAIRS)
-            direct, crossed = product_tiles(GROUP_ROWS * 2 * P)
-            direct = direct[:].rearrange("p (i c) -> p i c", i=GROUP_ROWS)
-            crossed = crossed[:].rearrange("p (i c) -> p i c", i=GROUP_ROWS)
-            for k in range(2):
-                cols = slice(P * k, P * (k + 1))
-                multiply(banks[k], cos_view, sin_view, direct[:, :, cols], crossed[:, :, cols])
-            if first_head == HEADS - 8 and g + 1 < GROUPS:
-                quantize(g + 1)
-            if duo < DUOS - VECTOR_ADDS:
-                add(nc.gpsimd, direct, crossed, g, slice(0, GROUP_ROWS), first_head, 2)
-                if duo >= DUOS - QUAD:
-                    store(g, first_head, 2)
-                elif duo % QUAD == QUAD - 1:
-                    store(g, first_head + 2 - HEADS // 2, HEADS // 2)
-            else:
-                left_over.append((direct, crossed, first_head))
+            plain = [k for k in range(2) if not summed_on_tensor(duo, k)]
+            banks = [turn_back(projected[k]) for k in plain]
+            if plain:
+                group_cols = slice(GROUP_ROWS * PAIRS * g, GROUP_ROWS * PAIRS * (g + 1))
+                cos_view = double_cos[:, group_cols, :].rearrange("p (i j) e -> p i j e", j=PAIRS)
+                sin_view = signed_sin[:, group_cols, :].rearrange("p (i j) e -> p i j e", j=PAIRS)
+                direct, crossed = product_tiles(GROUP_ROWS * len(plain) * P)
+                direct = direct[:].rearrange("p (i c) -> p i c", i=GROUP_ROWS)
+                crossed = crossed[:].rearrange("p (i c) -> p i c", i=GROUP_ROWS)
+                for k in plain:
+                    cols = slice(P * k, P * (k + 1))
+                    multiply(banks[k], cos_view, sin_view, direct[:, :, cols], crossed[:, :, cols])
+                if first_head == HEADS - 8 and g + 1 < GROUPS:
+                    quantize(g + 1)
+                combine(direct, crossed, g, slice(0, GROUP_ROWS), first_head, len(plain))
+            for k in range(len(plain), 2):
+                turn_and_sum(projected[k], g, first_head + k)
+                if duo >= DUOS - SUMMED_TAIL:
+                    store(g, first_head + k, 1)
+            if DUOS - QUAD <= duo < DUOS - SUMMED_TAIL:
+                store(g, first_head, 2)
+            elif duo < DUOS - QUAD and duo % QUAD == QUAD - 1:
+                store(g, first_head + 2 - HEADS // 2, HEADS // 2)
 
         turn_x(0, 0, PASSES)
         turn_x(1, 0, PASSES)
@@ -332,7 +400,9 @@ def tile_moonvitvisiontower_pa_kernel(
         half_rows = [(row, c) for row in range(GROUP_ROWS + 1, ROWS) for c in range(PASSES)]
         for duo in range(QUAD // 2, DUOS):
             g, first_head = divmod(2 * duo, HEADS)
-            ahead = [project(g, first_head + k) for k in range(2)]
+            ahead = [
+                (project_and_multiply if summed_on_tensor(duo, k) else project)(g, first_head + k) for k in range(2)
+            ]
             if duo < QUAD:
                 row = half_rows[0][0]
                 half_rows = half_rows[PASSES:]
@@ -340,19 +410,18 @@ def tile_moonvitvisiontower_pa_kernel(
             elif half_rows:
                 row, c = half_rows[0]
                 half_rows = half_rows[1:]
-                turn_x(row, c, 1)
-            if first_head == HEADS - 4 and g + 1 < GROUPS:
+                turn_sorted(row, c, sorted_words)
+            if duo >= QUAD - 1 and half_rows:
+                sorted_words = sort_words(*half_rows[0])
+            if first_head == HEADS - 8 and g + 1 < GROUPS:
                 repeat_cos(g + 1, nc.scalar.copy)
-            if first_head == HEADS - 2 and g + 1 < GROUPS:
+            if first_head == HEADS - 6 and g + 1 < GROUPS:
                 sign_sin_on_scalar(g + 1)
+            if first_head == HEADS - 2 and g + 1 < GROUPS:
+                turn_tables(g + 1)
             if duo == QUAD // 2:
                 finish_row(GROUP_ROWS - 1, biased)
             else:
                 finish_duo(duo - 1, biased)
             biased = ahead
         finish_duo(DUOS - 1, biased)
-        for direct, crossed, first_head in left_over:
-            for k in range(2):
-                cols = slice(P * k, P * (k + 1))
-                add(nc.vector, direct[:, :, cols], crossed[:, :, cols], GROUPS - 1, slice(0, GROUP_ROWS), first_head + k, 1)
-                store(GROUPS - 1, first_head + k, 1)

from contextlib import ExitStack

import concourse.mybir as mybir
from concourse.masks import make_identity

F32 = mybir.dt.float32
BF16 = mybir.dt.bfloat16
I32 = mybir.dt.int32
U32 = mybir.dt.uint32
U8 = mybir.dt.uint8
E5M2X4 = mybir.dt.float8_e5m2_x4
E2M1X4 = mybir.dt.float4_e2m1fn_x4
ALU = mybir.AluOpType
ACT = mybir.ActivationFunctionType

P = 128
TOKENS = 2048
D = 1024
CHANNELS = 2048
PASSES = 2
ROWS = TOKENS // P
GROUP_ROWS = 4
GROUPS = ROWS // GROUP_ROWS
GROUP_TOKENS = GROUP_ROWS * P
HEADS = CHANNELS // P
QUAD = 4
QUADS = HEADS // QUAD
STEPS = GROUPS * QUADS
PAIRS = P // 2
SUM_BANKS = 4
TURN_BANKS = 4
DUOS = GROUPS * HEADS // 2
SUMMED_TAIL = 2

FLOPS = 2 * TOKENS * D * CHANNELS


def tile_moonvitvisiontower_pa_kernel(
    tc, x, w_qk_words, w_qk_scales, b_qk, freqs_cos, freqs_sin, out_0, out_1
):
    nc = tc.nc
    x_rows = x.rearrange("(g p i) d -> g p i d", p=P, i=GROUP_ROWS)
    outs = [o.rearrange("(g p i) h d -> g p i (h d)", p=P, i=GROUP_ROWS) for o in (out_0, out_1)]

    with ExitStack() as ctx:
        keep = ctx.enter_context(tc.tile_pool(name="keep", bufs=1))
        work = ctx.enter_context(tc.tile_pool(name="work", bufs=2))
        psum = ctx.enter_context(tc.psum_pool(name="psum", bufs=1))
        ctx.enter_context(tc.manual_schedule())

        counters = {"sum": 0, "turn": 0}

        def next_bank(kind, banks, shape, dtype):
            n = counters[kind]
            counters[kind] = n + 1
            tag = "%s%d" % (kind, n % banks)
            return psum.tile(shape, dtype, name=tag, tag=tag)

        bias_rows = keep.tile([P, P], BF16)
        nc.gpsimd.memset(bias_rows[:], 0.0)
        ident_bf = keep.tile([P, P], BF16)
        make_identity(nc, ident_bf[:])
        ident = keep.tile([P, P], F32)
        make_identity(nc, ident[:])
        split = keep.tile([P, P], F32)
        nc.gpsimd.tensor_copy(
            out=split[:].rearrange("p (e j) -> p e j", e=2), in_=ident[:].rearrange("p (j e) -> p e j", e=2)
        )
        swap = keep.tile([P, P], F32)
        for e in range(2):
            nc.gpsimd.tensor_copy(out=swap[:, e:P:2], in_=ident[:, 1 - e : P : 2])
        w_scale = keep.tile([P, PASSES, CHANNELS], U8, align_bytes=64)
        nc.vector.memset(w_scale[:].rearrange("p g n -> p (g n)").bitcast(I32), 0)
        sign = keep.tile([P, 2], F32)
        nc.vector.memset(sign[:, 0:1], 1.0)
        nc.vector.memset(sign[:, 1:2], -1.0)

        nc.scalar.dma_start(out=bias_rows[0:HEADS, :], in_=b_qk.rearrange("(h c) -> h c", c=P))
        x_raw = []

        def load_row(i):
            t = keep.tile([P, 1, D], BF16, name="x_first%d" % i)
            nc.sync.dma_start(out=t[:], in_=x_rows[0, :, i : i + 1, :])
            x_raw.append(t[:, 0, :])

        load_row(0)
        load_row(1)
        for q in range(4):
            nc.sync.dma_start(
                out=w_scale[32 * q : 32 * q + 4, :, :].bitcast(I32),
                in_=w_qk_scales[:, 4 * q : 4 * q + 4, :].rearrange("g r n -> r g n").bitcast(I32),
            )
        quad_bytes = 2 * QUAD * P
        w_first = keep.tile([P, PASSES, quad_bytes], U8, align_bytes=64)
        nc.sync.dma_start(
            out=w_first[:].bitcast(I32),
            in_=w_qk_words[:, :, 0:quad_bytes].rearrange("g p n -> p g n").bitcast(I32),
        )
        sin = keep.tile([P, ROWS * PAIRS], BF16)
        nc.sync.dma_start(
            out=sin[:].rearrange("p (g c) -> p g c", g=GROUPS),
            in_=freqs_sin.rearrange("(g p i) j -> p g (i j)", p=P, i=GROUP_ROWS),
        )
        load_row(2)
        cos = keep.tile([P, ROWS * PAIRS], BF16)
        nc.sync.dma_start(
            out=cos[:].rearrange("p (g c) -> p g c", g=GROUPS),
            in_=freqs_cos.rearrange("(g p i) j -> p g (i j)", p=P, i=GROUP_ROWS),
        )
        load_row(3)
        w_tiles = [(0, w_first)]

        def load_w(first_head, heads):
            t = keep.tile([P, PASSES, 2 * P * heads], U8, name="w_from%d" % first_head, align_bytes=64)
            nc.sync.dma_start(
                out=t[:].bitcast(I32),
                in_=w_qk_words[:, :, 2 * P * first_head : 2 * P * (first_head + heads)]
                .rearrange("g p n -> p g n")
                .bitcast(I32),
            )
            w_tiles.append((first_head, t))

        def load_group(g):
            t = keep.tile([P, GROUP_ROWS, D], BF16, name="x_group%d" % g)
            nc.sync.dma_start(out=t[:], in_=x_rows[g])
            x_raw.extend(t[:, i, :] for i in range(GROUP_ROWS))

        load_w(QUAD, QUAD)
        load_group(1)
        load_w(2 * QUAD, 2 * QUAD)
        load_group(2)
        load_group(3)

        def w_words(g, head):
            first_head, t = [entry for entry in w_tiles if entry[0] <= head][-1]
            return t[:, g, 2 * P * (head - first_head) : 2 * P * (head - first_head + 1)]

        bias_psum = next_bank("sum", SUM_BANKS, [P, P], BF16)
        nc.tensor.transpose(bias_psum[:], bias_rows[:], ident_bf[:])
        bias = keep.tile([P, HEADS], F32)
        nc.scalar.activation(out=bias[:], in_=bias_psum[:, 0:HEADS], func=ACT.Identity)

        grouped = {}
        codes = {}
        scales = {}
        signed_sin = keep.tile([P, ROWS * PAIRS, 2], BF16)
        double_cos = keep.tile([P, ROWS * PAIRS, 2], BF16)

        def turn_x(row, first_pass, passes):
            g, i = divmod(row, GROUP_ROWS)
            if i == 0 and first_pass == 0:
                grouped[g] = work.tile([P, PASSES, GROUP_TOKENS, 2], F32, name="grouped", align_bytes=64)
            words = x_raw[row].bitcast(F32)
            bank = next_bank("sum", SUM_BANKS, [P, passes, 2, P], F32)
            for c in range(passes):
                first = 256 * (first_pass + c)
                for u in range(2):
                    nc.tensor.transpose(bank[:, c, u, :], words[:, first + u : first + 256 : 2], ident[:])
            nc.scalar.copy(
                out=grouped[g][:, first_pass : first_pass + passes, P * i : P * (i + 1), :],
                in_=bank[:].rearrange("p c u r -> p c r u"),
            )

        def sort_words(row, c):
            words = x_raw[row].bitcast(F32)[:, 256 * c : 256 * (c + 1)]
            sorted_words = work.tile([P, 2, P], F32, name="sorted_words", bufs=3)
            nc.scalar.copy(out=sorted_words[:], in_=words.rearrange("p (k u) -> p u k", u=2))
            return sorted_words

        def turn_sorted(row, c, sorted_words):
            g, i = divmod(row, GROUP_ROWS)
            if i == 0 and c == 0:
                grouped[g] = work.tile([P, PASSES, GROUP_TOKENS, 2], F32, name="grouped", align_bytes=64)
            bank = next_bank("sum", SUM_BANKS, [P, 2, P], F32)
            for u in range(2):
                nc.tensor.transpose(bank[:, u, :], sorted_words[:, u, :], ident[:])
            nc.scalar.copy(out=grouped[g][:, c, P * i : P * (i + 1), :], in_=bank[:].rearrange("p u r -> p r u"))

        def new_codes(g):
            codes[g] = work.tile([P, PASSES, GROUP_TOKENS], U32, name="codes", align_bytes=64)
            scales[g] = work.tile([P, PASSES, GROUP_TOKENS], U8, name="scales", align_bytes=64)

        def quantize(g):
            new_codes(g)
            nc.vector.quantize_mx(
                out=codes[g][:].rearrange("p c r -> p (c r)").bitcast(E5M2X4),
                scales=scales[g][:].rearrange("p c r -> p (c r)"),
                in_=grouped[g][:].rearrange("p c r u -> p (c r u)").bitcast(BF16),
            )

        def quantize_row(i):
            if i == 0:
                new_codes(0)
            cols = slice(P * i, P * (i + 1))
            for c in range(PASSES):
                nc.vector.quantize_mx(
                    out=codes[0][:, c, cols].bitcast(E5M2X4),
                    scales=scales[0][:, c, cols],
                    in_=grouped[0][:, c, cols, :].rearrange("p r u -> p (r u)").bitcast(BF16),
                )

        def sign_sin(g):
            cols = slice(GROUP_ROWS * PAIRS * g, GROUP_ROWS * PAIRS * (g + 1))
            shape = [P, GROUP_ROWS * PAIRS, 2]
            nc.vector.tensor_tensor(
                out=signed_sin[:, cols, :],
                in0=sin[:, cols].unsqueeze(2).to_broadcast(shape),
                in1=sign[:].unsqueeze(1).to_broadcast(shape),
                op=ALU.mult,
            )

        def sign_sin_on_scalar(g):
            cols = slice(GROUP_ROWS * PAIRS * g, GROUP_ROWS * PAIRS * (g + 1))
            nc.scalar.copy(out=signed_sin[:, cols, 0], in_=sin[:, cols])
            nc.scalar.activation(out=signed_sin[:, cols, 1], in_=sin[:, cols], func=ACT.Copy, scale=-1.0)

        def repeat_cos(g, copy):
            cols = slice(GROUP_ROWS * PAIRS * g, GROUP_ROWS * PAIRS * (g + 1))
            copy(out=double_cos[:, cols, :], in_=cos[:, cols].unsqueeze(2).to_broadcast([P, GROUP_ROWS * PAIRS, 2]))

        def mx_group(out, g, head, cols):
            for c in range(PASSES):
                nc.tensor.matmul_mx(
                    out=out,
                    lhsT=w_words(c, head).bitcast(E2M1X4),
                    lhsT_scale=w_scale[:, c, P * head : P * (head + 1)],
                    rhs=codes[g][:, c, cols].bitcast(E5M2X4),
                    rhs_scale=scales[g][:, c, cols],
                    start=(c == 0),
                    stop=(c == PASSES - 1),
                )

        def add_bias(out, in_, head):
            nc.scalar.activation(out=out, in_=in_, func=ACT.Identity, bias=bias[:, head : head + 1])

        turned_tables = {}

        def turn_tables(g):
            bank = next_bank("sum", SUM_BANKS, [P, 2, GROUP_ROWS, P], BF16)
            for n, table in enumerate((double_cos, signed_sin)):
                for i in range(GROUP_ROWS):
                    row = GROUP_ROWS * g + i
                    nc.tensor.transpose(
                        bank[:, n, i, :],
                        table[:, PAIRS * row : PAIRS * (row + 1), :].rearrange("p j e -> p (j e)"),
                        ident_bf[:],
                    )
            turned_tables[g] = work.tile([P, 2, GROUP_TOKENS], BF16, name="turned_table")
            nc.scalar.copy(out=turned_tables[g][:], in_=bank[:].rearrange("p n i r -> p n (i r)"))

        def summed_on_tensor(duo, k):
            return duo >= DUOS - SUMMED_TAIL or (duo >= HEADS // 2 and duo % 2 == 1 and k == 1)

        def project_and_multiply(g, head):
            bank = next_bank("sum", SUM_BANKS, [P, GROUP_TOKENS], F32)
            mx_group(bank[:], g, head, slice(0, GROUP_TOKENS))
            products = work.tile([P, 2, GROUP_TOKENS], F32, name="products", bufs=4)
            for n in range(2):
                nc.vector.scalar_tensor_tensor(
                    out=products[:, n, :],
                    in0=bank[:],
                    scalar=bias[:, head : head + 1],
                    in1=turned_tables[g][:, n, :],
                    op0=ALU.add,
                    op1=ALU.mult,
                )
            return products

        def project(g, head):
            bank = next_bank("sum", SUM_BANKS, [P, GROUP_TOKENS], F32)
            mx_group(bank[:], g, head, slice(0, GROUP_TOKENS))
            biased = work.tile([P, GROUP_TOKENS], F32, name="biased", bufs=6)
            add_bias(biased[:], bank[:], head)
            return biased

        def project_row(i):
            bank = next_bank("sum", SUM_BANKS, [P, QUAD * P], F32)
            for head in range(QUAD):
                mx_group(bank[:, P * head : P * (head + 1)], 0, head, slice(P * i, P * (i + 1)))
            biased = work.tile([P, QUAD * P], F32, name="biased", bufs=6)
            for head in range(QUAD):
                add_bias(biased[:, P * head : P * (head + 1)], bank[:, P * head : P * (head + 1)], head)
            return biased

        def turn_back(biased):
            bank = next_bank("turn", TURN_BANKS, [P, 4, P], F32)
            for i in range(4):
                nc.tensor.transpose(bank[:, i, :], biased[:, P * i : P * (i + 1)], split[:])
            return bank

        pair_shape = [P, 4, PAIRS, 2]

        def multiply(bank, cos_view, sin_view, direct, crossed):
            pairs = bank[:].rearrange("p i (e j) -> p i j e", e=2)
            nc.vector.tensor_tensor(
                out=direct.rearrange("p i (j e) -> p i j e", e=2), in0=pairs, in1=cos_view, op=ALU.mult
            )
            nc.vector.tensor_tensor(
                out=crossed.rearrange("p i (j e) -> p i j e", e=2),
                in0=pairs[:, :, :, ::-1],
                in1=sin_view,
                op=ALU.mult,
            )

        def product_tiles(width):
            direct = work.tile([P, width], F32, name="direct", bufs=5)
            crossed = work.tile([P, width], F32, name="crossed", bufs=5)
            return direct, crossed

        results = {}

        def result_view(g, rows, first_head, heads):
            which, head = divmod(first_head, HEADS // 2)
            if (g, which) not in results:
                results[(g, which)] = work.tile([P, GROUP_ROWS, D], F32, name="result", bufs=3)
            return results[(g, which)][:, rows, P * head : P * (head + heads)]

        def combine(direct, crossed, g, rows, first_head, heads):
            nc.gpsimd.tensor_tensor(
                out=result_view(g, rows, first_head, heads), in0=direct, in1=crossed, op=ALU.subtract
            )

        def turn_and_sum(products, g, head):
            bank = next_bank("turn", TURN_BANKS, [P, GROUP_ROWS, P], F32)
            for i in range(GROUP_ROWS):
                for n, order in enumerate((ident, swap)):
                    nc.tensor.matmul(
                        out=bank[:, i, :],
                        lhsT=products[:, n, P * i : P * (i + 1)],
                        rhs=order[:],
                        start=(n == 0),
                        stop=(n == 1),
                        is_transpose=True,
                    )
            nc.scalar.copy(out=result_view(g, slice(0, GROUP_ROWS), head, 1), in_=bank[:])

        def store(g, first_head, heads):
            which, head = divmod(first_head, HEADS // 2)
            cols = slice(P * head, P * (head + heads))
            nc.sync.dma_start(out=outs[which][g, :, :, cols], in_=results[(g, which)][:, :, cols])

        def finish_row(i, biased):
            bank = turn_back(biased)
            direct, crossed = product_tiles(QUAD * P)
            row_cols = slice(PAIRS * i, PAIRS * (i + 1))
            multiply(
                bank,
                double_cos[:, row_cols, :].unsqueeze(1).to_broadcast(pair_shape),
                signed_sin[:, row_cols, :].unsqueeze(1).to_broadcast(pair_shape),
                direct[:].rearrange("p (h c) -> p h c", c=P),
                crossed[:].rearrange("p (h c) -> p h c", c=P),
            )
            combine(direct[:].unsqueeze(1), crossed[:].unsqueeze(1), 0, slice(i, i + 1), 0, QUAD)

        def finish_duo(duo, projected):
            g, first_head = divmod(2 * duo, HEADS)
            plain = [k for k in range(2) if not summed_on_tensor(duo, k)]
            banks = [turn_back(projected[k]) for k in plain]
            if plain:
                group_cols = slice(GROUP_ROWS * PAIRS * g, GROUP_ROWS * PAIRS * (g + 1))
                cos_view = double_cos[:, group_cols, :].rearrange("p (i j) e -> p i j e", j=PAIRS)
                sin_view = signed_sin[:, group_cols, :].rearrange("p (i j) e -> p i j e", j=PAIRS)
                direct, crossed = product_tiles(GROUP_ROWS * len(plain) * P)
                direct = direct[:].rearrange("p (i c) -> p i c", i=GROUP_ROWS)
                crossed = crossed[:].rearrange("p (i c) -> p i c", i=GROUP_ROWS)
                for k in plain:
                    cols = slice(P * k, P * (k + 1))
                    multiply(banks[k], cos_view, sin_view, direct[:, :, cols], crossed[:, :, cols])
                if first_head == HEADS - 8 and g + 1 < GROUPS:
                    quantize(g + 1)
                combine(direct, crossed, g, slice(0, GROUP_ROWS), first_head, len(plain))
            for k in range(len(plain), 2):
                turn_and_sum(projected[k], g, first_head + k)
                if duo >= DUOS - SUMMED_TAIL:
                    store(g, first_head + k, 1)
            if DUOS - QUAD <= duo < DUOS - SUMMED_TAIL:
                store(g, first_head, 2)
            elif duo < DUOS - QUAD and duo % QUAD == QUAD - 1:
                store(g, first_head + 2 - HEADS // 2, HEADS // 2)

        turn_x(0, 0, PASSES)
        turn_x(1, 0, PASSES)
        quantize_row(0)
        quantize_row(1)
        sign_sin(0)
        repeat_cos(0, nc.vector.tensor_copy)
        biased = project_row(0)
        turn_x(2, 0, PASSES)
        quantize_row(2)
        finish_row(0, biased)
        biased = project_row(1)
        turn_x(3, 0, PASSES)
        quantize_row(3)
        for i in range(2, GROUP_ROWS):
            ahead = project_row(i)
            finish_row(i - 1, biased)
            biased = ahead
        turn_x(GROUP_ROWS, 0, PASSES)

        half_rows = [(row, c) for row in range(GROUP_ROWS + 1, ROWS) for c in range(PASSES)]
        for duo in range(QUAD // 2, DUOS):
            g, first_head = divmod(2 * duo, HEADS)
            ahead = [
                (project_and_multiply if summed_on_tensor(duo, k) else project)(g, first_head + k) for k in range(2)
            ]
            if duo < QUAD:
                row = half_rows[0][0]
                half_rows = half_rows[PASSES:]
                turn_x(row, 0, PASSES)
            elif half_rows:
                row, c = half_rows[0]
                half_rows = half_rows[1:]
                turn_sorted(row, c, sorted_words)
            if duo >= QUAD - 1 and half_rows:
                sorted_words = sort_words(*half_rows[0])
            if first_head == HEADS - 8 and g + 1 < GROUPS:
                repeat_cos(g + 1, nc.scalar.copy)
            if first_head == HEADS - 6 and g + 1 < GROUPS:
                sign_sin_on_scalar(g + 1)
            if first_head == HEADS - 2 and g + 1 < GROUPS:
                turn_tables(g + 1)
            if duo == QUAD // 2:
                finish_row(GROUP_ROWS - 1, biased)
            else:
                finish_duo(duo - 1, biased)
            biased = ahead
        finish_duo(DUOS - 1, biased)
